import numpy as np
import ml_dtypes


def mxq(x, axis, fmt="e4m3"):
    dtype, down = {"e4m3": (ml_dtypes.float8_e4m3fn, 7), "e5m2": (ml_dtypes.float8_e5m2, 14)}[fmt]
    v = np.moveaxis(np.asarray(x, np.float32).astype(ml_dtypes.bfloat16).astype(np.float64), axis, -1)
    blocks = v.reshape(v.shape[:-1] + (-1, 32))
    amax = np.abs(blocks).max(-1, keepdims=True)
    byte = np.maximum(np.where(amax > 0, np.frexp(amax)[1] - 1 + 127, 0) - down, 1)
    scale = np.exp2(byte - 127.0)
    codes = (blocks / scale).astype(np.float32).astype(dtype).astype(np.float64)
    return np.moveaxis((codes * scale).reshape(v.shape), -1, axis)


WIDE = False


def mx_kscale(k):
    if not WIDE:
        return np.ones(k)
    levels = np.array([20, -20, 10, -10, 0])
    a = np.random.permutation(np.resize(levels, k // 512 * 4)).reshape(k // 512, 4)
    idx = np.arange(k)
    return np.exp2(a[idx // 512, idx % 128 // 32])


BF16 = ml_dtypes.bfloat16


def bf(x):
    return np.asarray(x, np.float32).astype(BF16)


def f64(x):
    return np.asarray(x).astype(np.float64)


B, S, D_IN, D_OUT = 2, 512, 2048, 2048
THRESHOLD = 0.5


def ternarize(w, threshold=THRESHOLD):
    mag = np.abs(w)
    mask = np.where(mag > threshold, 1.0, 0.0)
    cnt = np.sum(mask)
    ssum = np.sum(mag * mask)
    scale = np.where(cnt > 0, ssum / np.maximum(cnt, 1.0), 1.0)
    return np.sign(w) * mask * scale


def setup_inputs():
    s = mx_kscale(D_OUT)
    t = np.maximum(s, 1.0) ** 2
    x = np.random.standard_normal((B, S, D_IN)) * 2.0 / np.sqrt(D_IN)
    weight = np.random.standard_normal((D_OUT, D_IN)) / t[:, None]
    bias = np.random.standard_normal(D_OUT) * 0.3
    g = np.random.standard_normal((B, S, D_OUT)) * np.exp2(np.random.randint(-12, 1, (B, S, 1))) * t
    return {"x": bf(x), "weight": bf(weight), "bias": bf(bias), "grad_out": bf(g)}


def reference(x, weight, bias, grad_out):
    w_t = ternarize(f64(weight))
    return mxq(f64(grad_out), 2, "e5m2") @ mxq(w_t, 0, "e4m3")

@@ -1,0 +1,236 @@
+from contextlib import ExitStack
+
+import concourse.mybir as mybir
+from concourse.masks import make_identity
+
+FLOPS = 2 * 1024 * 2048 * 2048
+BYTES = 2048 * 2048 * 2 + 1024 * 2048 * 2 + 1024 * 2048 * 4
+
+BF16 = mybir.dt.bfloat16
+F32 = mybir.dt.float32
+I32 = mybir.dt.int32
+U32 = mybir.dt.uint32
+U8 = mybir.dt.uint8
+E4 = mybir.dt.float8_e4m3fn_x4
+E5 = mybir.dt.float8_e5m2_x4
+ALU = mybir.AluOpType
+ACT = mybir.ActivationFunctionType
+AX = mybir.AxisListType
+
+P = 128
+D = 2048
+NPASS = 4
+NBLK = 4
+MT = 8
+SUB = 1024
+S_COLS = [640, 512]
+V_REGROUP = 288
+ABS_MASK = 0x7FFF7FFF
+SIGN_MASK = -2147450880
+
+
+def tile_ternarylinear_kernel(tc, x, weight, bias, grad_out, out):
+    nc = tc.nc
+    wv = weight.rearrange("(c u p e) d -> c u p e d", c=NPASS, u=2, p=P, e=2)
+    gflat = grad_out.flatten_outer_dims()
+    oflat = out.flatten_outer_dims()
+
+    with ExitStack() as ctx:
+        keep = ctx.enter_context(tc.tile_pool(name="keep", bufs=1))
+        gpool = ctx.enter_context(tc.tile_pool(name="gpool", bufs=3))
+        ggpool = ctx.enter_context(tc.tile_pool(name="ggpool", bufs=2))
+        psum = ctx.enter_context(tc.psum_pool(name="psum", bufs=1))
+
+        w_sb = []
+        t_sb = []
+        for c in range(NPASS):
+            w_c = keep.tile([P, 4, D], BF16, name="w%d" % c)
+            t_c = keep.tile([P, 4, D], BF16, name="t%d" % c)
+            w_sb.append(w_c)
+            t_sb.append(t_c)
+        for c in range(NPASS):
+            for u in range(2):
+                nc.sync.dma_start(out=w_sb[c][:, 2 * u : 2 * u + 2, :], in_=wv[c, u])
+
+        wcodes = keep.tile([P, NBLK, NPASS, 512], U32, align_bytes=64, name="wcodes")
+        wscale = keep.tile([P, NBLK, NPASS, 512], U8, align_bytes=64, name="wscale")
+        gcodes = keep.tile([P, MT, 512], U32, align_bytes=64, name="gcodes")
+        gscale = keep.tile([P, MT, 512], U8, align_bytes=64, name="gscale")
+
+        ident = keep.tile([P, P], F32, name="ident")
+        make_identity(nc, ident[:])
+        ones_f = keep.tile([P, P], F32, name="ones_f")
+        nc.vector.memset(ones_f[:], 1.0)
+        ones_b = keep.tile([P, 32], BF16, name="ones_b")
+        nc.vector.memset(ones_b[:], 1.0)
+        neghalf = keep.tile([P, 1], F32, name="neghalf")
+        nc.vector.memset(neghalf[:], -0.5)
+        n_sub = NPASS * 2 * (D // SUB)
+        racc = keep.tile([P, n_sub], F32, name="racc")
+        stat = keep.tile([P, 4], F32, name="stat")
+        nc.vector.memset(stat[:], 0.0)
+
+        cnt_ps = psum.tile([P, 32], F32, tag="b0", name="cnt_ps")
+        mag_ps = psum.tile([P, 32], F32, tag="b1", name="mag_ps")
+
+        subs = [(c, u, h) for c in range(NPASS) for u in range(2) for h in range(D // SUB)]
+        n_v = 0
+        with tc.tile_pool(name="apool", bufs=3) as apool, tc.tile_pool(name="mxpool", bufs=2) as mxpool:
+            for i, (c, u, h) in enumerate(subs):
+                ss = S_COLS[i % 2]
+                vs = SUB - ss
+                n_v += P * 2 * vs
+                cols = slice(SUB * h, SUB * h + SUB)
+                rows = slice(2 * u, 2 * u + 2)
+                a = apool.tile([P, 2, SUB], BF16, name="a")
+                nc.vector.tensor_scalar(
+                    out=a[:].bitcast(I32),
+                    in0=w_sb[c][:, rows, cols].bitcast(I32),
+                    scalar1=ABS_MASK,
+                    scalar2=None,
+                    op0=ALU.bitwise_and,
+                )
+                junk = mxpool.tile([P, 2, 640], BF16, name="junk")
+                nc.scalar.activation(
+                    out=junk[:, :, 0:ss],
+                    in_=a[:, :, 0:ss],
+                    func=ACT.Relu,
+                    bias=neghalf[:, 0:1],
+                    scale=1.0,
+                    accum_out=racc[:, i : i + 1],
+                )
+                mx = mxpool.tile([P, 2, 512], BF16, name="mx")
+                nc.vector.tensor_scalar(
+                    out=mx[:, :, 0:vs], in0=a[:, :, ss:SUB], scalar1=0.5, scalar2=None, op0=ALU.max
+                )
+                nc.vector.tensor_scalar(
+                    out=t_sb[c][:, rows, cols], in0=a[:], scalar1=0.5, scalar2=None, op0=ALU.is_gt
+                )
+                for e in range(2):
+                    for j in range(SUB // P):
+                        nc.tensor.matmul(
+                            cnt_ps[:],
+                            lhsT=t_sb[c][:, 2 * u + e, SUB * h + P * j : SUB * h + P * j + P],
+                            rhs=ones_b[:],
+                            start=(i == 0 and e == 0 and j == 0),
+                            stop=(i == n_sub - 1 and e == 1 and j == SUB // P - 1),
+                        )
+                for e in range(2):
+                    for j in range(vs // P):
+                        nc.tensor.matmul(
+                            mag_ps[:],
+                            lhsT=mx[:, e, P * j : P * j + P],
+                            rhs=ones_b[:],
+                            start=(i == 0 and e == 0 and j == 0),
+                            stop=(i == n_sub - 1 and e == 1 and j == vs // P - 1),
+                        )
+
+        nc.vector.tensor_copy(out=stat[:, 0:1], in_=cnt_ps[:, 0:1])
+        nc.vector.tensor_copy(out=stat[:, 1:2], in_=mag_ps[:, 0:1])
+        nc.vector.tensor_reduce(out=stat[:, 2:3], in_=racc[:], axis=AX.X, op=ALU.add)
+        tot_ps = psum.tile([P, 4], F32, tag="b2", name="tot_ps")
+        nc.tensor.matmul(tot_ps[:], lhsT=ones_f[:], rhs=stat[:], start=True, stop=True)
+        tot = keep.tile([P, 4], F32, name="tot")
+        nc.vector.tensor_copy(out=tot[:], in_=tot_ps[:])
+        sm = keep.tile([P, 8], F32, name="sm")
+        nc.vector.tensor_scalar(out=sm[:, 0:1], in0=tot[:, 0:1], scalar1=1.0, scalar2=None, op0=ALU.max)
+        nc.vector.reciprocal(out=sm[:, 1:2], in_=sm[:, 0:1])
+        nc.vector.tensor_tensor(out=sm[:, 2:3], in0=tot[:, 1:2], in1=tot[:, 2:3], op=ALU.add)
+        nc.vector.scalar_tensor_tensor(
+            out=sm[:, 3:4], in0=tot[:, 0:1], scalar=0.5, in1=sm[:, 2:3], op0=ALU.mult, op1=ALU.add
+        )
+        nc.vector.scalar_tensor_tensor(
+            out=sm[:, 4:5], in0=sm[:, 3:4], scalar=-0.5 * n_v, in1=sm[:, 1:2], op0=ALU.add, op1=ALU.mult
+        )
+        nc.vector.scalar_tensor_tensor(
+            out=sm[:, 5:6], in0=tot[:, 0:1], scalar=0.0, in1=sm[:, 4:5], op0=ALU.is_equal, op1=ALU.add
+        )
+        s_ap = sm[:, 5:6]
+
+        for m in range(MT):
+            g = gpool.tile([P, D], BF16, name="g")
+            nc.sync.dma_start(out=g[:], in_=gflat[P * m : P * m + P, :])
+            gw = g[:].bitcast(F32)
+            gg = ggpool.tile([P, NPASS, P, 4], BF16, align_bytes=64, name="gg")
+            ggf = gg[:].bitcast(F32)
+            for h in range(2):
+                xt = psum.tile([P, 2, 2, P], F32, tag="b%d" % (4 + (2 * m + h) % 4), name="xt")
+                for cc in range(2):
+                    for u in range(2):
+                        w0 = 256 * (2 * h + cc) + P * u
+                        nc.tensor.transpose(xt[:, cc, u, :], gw[:, w0 : w0 + P], ident[:])
+                nc.scalar.copy(
+                    out=ggf[:, 2 * h : 2 * h + 2, :, :], in_=xt[:].rearrange("p c u r -> p c r u")
+                )
+            nc.vector.quantize_mx(
+                out=gcodes[:, m, :].bitcast(E5),
+                scales=gscale[:, m, :],
+                in_=gg[:].rearrange("p c r t -> p (c r t)"),
+            )
+
+        post = ctx.enter_context(tc.tile_pool(name="post", bufs=3))
+        opool = ctx.enter_context(tc.tile_pool(name="opool", bufs=6))
+
+        def make_chunk(n, c):
+            cols = slice(512 * n, 512 * n + 512)
+            tv = t_sb[c][:, :, cols].bitcast(I32)
+            nc.vector.scalar_tensor_tensor(
+                out=tv,
+                in0=w_sb[c][:, :, cols].bitcast(I32),
+                scalar=SIGN_MASK,
+                in1=tv,
+                op0=ALU.bitwise_and,
+                op1=ALU.bitwise_or,
+            )
+            grp = post.tile([P, 512, 4], BF16, align_bytes=64, name="grp")
+            src = t_sb[c][:, :, cols]
+            vc = V_REGROUP
+            nc.vector.tensor_scalar(
+                out=grp[:, 0:vc, :].rearrange("p (c i) t -> p c t i", i=4),
+                in0=src[:, :, 0:vc].rearrange("p t (c i) -> p c t i", i=4),
+                scalar1=s_ap,
+                scalar2=None,
+                op0=ALU.mult,
+            )
+            nc.scalar.activation(
+                out=grp[:, vc:512, :].rearrange("p (c i) t -> p c t i", i=4),
+                in_=src[:, :, vc:512].rearrange("p t (c i) -> p c t i", i=4),
+                func=ACT.Copy,
+                scale=s_ap,
+            )
+            nc.vector.quantize_mx(
+                out=wcodes[:, n, c, :].bitcast(E4),
+                scales=wscale[:, n, c, :],
+                in_=grp[:].rearrange("p w t -> p (w t)"),
+            )
+
+        def mx_pass(acc, m, n, c):
+            nc.tensor.matmul_mx(
+                out=acc[:],
+                lhsT=gcodes[:, m, P * c : P * c + P].bitcast(E5),
+                lhsT_scale=gscale[:, m, P * c : P * c + P],
+                rhs=wcodes[:, n, c, :].bitcast(E4),
+                rhs_scale=wscale[:, n, c, :],
+                start=(c == 0),
+                stop=(c == NPASS - 1),
+            )
+
+        def finish(acc, m, n):
+            o = opool.tile([P, 512], F32, name="o")
+            nc.scalar.copy(out=o[:], in_=acc[:])
+            nc.sync.dma_start(out=oflat[P * m : P * m + P, 512 * n : 512 * n + 512], in_=o[:])
+
+        for n in range(NBLK):
+            groups = [range(0, 4), range(4, 8)] if n == 0 else [range(0, 8)]
+            for gi, ms in enumerate(groups):
+                accs = {}
+                for m in ms:
+                    acc = psum.tile([P, 512], F32, tag="b%d" % m, name="acc")
+                    accs[m] = acc
+                for c in range(NPASS):
+                    if gi == 0:
+                        make_chunk(n, c)
+                    for m in ms:
+                        mx_pass(accs[m], m, n, c)
+                for m in ms:
+                    finish(accs[m], m, n)

@@ -21,23 +21,34 @@ P = 128
 D = 2048
 NPASS = 4
 NBLK = 4
+NCHUNK = 16
 MT = 8
-SUB = 1024
-S_COLS = [640, 512]
-V_REGROUP = 288
+NARROW = 8
 ABS_MASK = 0x7FFF7FFF
 SIGN_MASK = -2147450880
+PIECES = (
+    [(0, 0, 0, 1024), (0, 0, 1024, 1024)]
+    + [(c, u, 0, 2048) for c in range(4) for u in range(2) if (c, u) not in ((0, 0), (3, 1))]
+    + [(3, 1, 0, 1024), (3, 1, 1024, 512), (3, 1, 1536, 512)]
+)
+S_BLOCKS = {2048: 4, 1024: 2, 512: 1}
+V_COLS_RAMP = 192
+V_COLS = 128
+LA_T = 3
+LA_S = 2
+LA_V = 1
+G_BANK = [(3, 4), (5, 6), (7, 3), (4, 5), (6, 7), (4, 5), (6, 7), (6, 7)]
 
 
 def tile_ternarylinear_kernel(tc, x, weight, bias, grad_out, out):
     nc = tc.nc
     wv = weight.rearrange("(c u p e) d -> c u p e d", c=NPASS, u=2, p=P, e=2)
-    gflat = grad_out.flatten_outer_dims()
+    gv = grad_out.flatten_outer_dims().rearrange("(q t p) d -> q p t d", t=2, p=P)
     oflat = out.flatten_outer_dims()
 
     with ExitStack() as ctx:
         keep = ctx.enter_context(tc.tile_pool(name="keep", bufs=1))
-        gpool = ctx.enter_context(tc.tile_pool(name="gpool", bufs=3))
+        share = ctx.enter_context(tc.tile_pool(name="share", bufs=3))
         ggpool = ctx.enter_context(tc.tile_pool(name="ggpool", bufs=2))
         psum = ctx.enter_context(tc.psum_pool(name="psum", bufs=1))
 
@@ -48,11 +59,22 @@ def tile_ternarylinear_kernel(tc, x, weight, bias, grad_out, out):
             t_c = keep.tile([P, 4, D], BF16, name="t%d" % c)
             w_sb.append(w_c)
             t_sb.append(t_c)
-        for c in range(NPASS):
-            for u in range(2):
-                nc.sync.dma_start(out=w_sb[c][:, 2 * u : 2 * u + 2, :], in_=wv[c, u])
+        for c, u, c0, ncol in PIECES:
+            nc.sync.dma_start(
+                out=w_sb[c][:, 2 * u : 2 * u + 2, c0 : c0 + ncol], in_=wv[c, u][:, :, c0 : c0 + ncol]
+            )
+        g_sb = []
+        for q in range(4):
+            if q < 3:
+                g_q = share.tile([P, 2, D], BF16, tag="x", align_bytes=64, name="g%d" % q)
+            else:
+                g_q = keep.tile([P, 2, D], BF16, name="g3")
+            nc.sync.dma_start(out=g_q[:], in_=gv[q])
+            g_sb.append(g_q)
 
-        wcodes = keep.tile([P, NBLK, NPASS, 512], U32, align_bytes=64, name="wcodes")
+        wcodes = {}
+        wcodes0 = keep.tile([P, NPASS, 512], U32, align_bytes=64, name="wcodes0")
+        wcodes[0] = wcodes0
         wscale = keep.tile([P, NBLK, NPASS, 512], U8, align_bytes=64, name="wscale")
         gcodes = keep.tile([P, MT, 512], U32, align_bytes=64, name="gcodes")
         gscale = keep.tile([P, MT, 512], U8, align_bytes=64, name="gscale")
@@ -65,113 +87,52 @@ def tile_ternarylinear_kernel(tc, x, weight, bias, grad_out, out):
         nc.vector.memset(ones_b[:], 1.0)
         neghalf = keep.tile([P, 1], F32, name="neghalf")
         nc.vector.memset(neghalf[:], -0.5)
-        n_sub = NPASS * 2 * (D // SUB)
-        racc = keep.tile([P, n_sub], F32, name="racc")
+        n_pc = len(PIECES)
+        racc = keep.tile([P, n_pc], F32, name="racc")
         stat = keep.tile([P, 4], F32, name="stat")
         nc.vector.memset(stat[:], 0.0)
-
-        cnt_ps = psum.tile([P, 32], F32, tag="b0", name="cnt_ps")
-        mag_ps = psum.tile([P, 32], F32, tag="b1", name="mag_ps")
-
-        subs = [(c, u, h) for c in range(NPASS) for u in range(2) for h in range(D // SUB)]
-        n_v = 0
-        with tc.tile_pool(name="apool", bufs=3) as apool, tc.tile_pool(name="mxpool", bufs=2) as mxpool:
-            for i, (c, u, h) in enumerate(subs):
-                ss = S_COLS[i % 2]
-                vs = SUB - ss
-                n_v += P * 2 * vs
-                cols = slice(SUB * h, SUB * h + SUB)
-                rows = slice(2 * u, 2 * u + 2)
-                a = apool.tile([P, 2, SUB], BF16, name="a")
-                nc.vector.tensor_scalar(
-                    out=a[:].bitcast(I32),
-                    in0=w_sb[c][:, rows, cols].bitcast(I32),
-                    scalar1=ABS_MASK,
-                    scalar2=None,
-                    op0=ALU.bitwise_and,
-                )
-                junk = mxpool.tile([P, 2, 640], BF16, name="junk")
-                nc.scalar.activation(
-                    out=junk[:, :, 0:ss],
-                    in_=a[:, :, 0:ss],
-                    func=ACT.Relu,
-                    bias=neghalf[:, 0:1],
-                    scale=1.0,
-                    accum_out=racc[:, i : i + 1],
-                )
-                mx = mxpool.tile([P, 2, 512], BF16, name="mx")
-                nc.vector.tensor_scalar(
-                    out=mx[:, :, 0:vs], in0=a[:, :, ss:SUB], scalar1=0.5, scalar2=None, op0=ALU.max
-                )
-                nc.vector.tensor_scalar(
-                    out=t_sb[c][:, rows, cols], in0=a[:], scalar1=0.5, scalar2=None, op0=ALU.is_gt
-                )
-                for e in range(2):
-                    for j in range(SUB // P):
-                        nc.tensor.matmul(
-                            cnt_ps[:],
-                            lhsT=t_sb[c][:, 2 * u + e, SUB * h + P * j : SUB * h + P * j + P],
-                            rhs=ones_b[:],
-                            start=(i == 0 and e == 0 and j == 0),
-                            stop=(i == n_sub - 1 and e == 1 and j == SUB // P - 1),
-                        )
-                for e in range(2):
-                    for j in range(vs // P):
-                        nc.tensor.matmul(
-                            mag_ps[:],
-                            lhsT=mx[:, e, P * j : P * j + P],
-                            rhs=ones_b[:],
-                            start=(i == 0 and e == 0 and j == 0),
-                            stop=(i == n_sub - 1 and e == 1 and j == vs // P - 1),
-                        )
-
-        nc.vector.tensor_copy(out=stat[:, 0:1], in_=cnt_ps[:, 0:1])
-        nc.vector.tensor_copy(out=stat[:, 1:2], in_=mag_ps[:, 0:1])
-        nc.vector.tensor_reduce(out=stat[:, 2:3], in_=racc[:], axis=AX.X, op=ALU.add)
-        tot_ps = psum.tile([P, 4], F32, tag="b2", name="tot_ps")
-        nc.tensor.matmul(tot_ps[:], lhsT=ones_f[:], rhs=stat[:], start=True, stop=True)
-        tot = keep.tile([P, 4], F32, name="tot")
-        nc.vector.tensor_copy(out=tot[:], in_=tot_ps[:])
+        st = keep.tile([P, 8], F32, name="st")
+        scr = keep.tile([P, P], F32, name="scr")
         sm = keep.tile([P, 8], F32, name="sm")
-        nc.vector.tensor_scalar(out=sm[:, 0:1], in0=tot[:, 0:1], scalar1=1.0, scalar2=None, op0=ALU.max)
-        nc.vector.reciprocal(out=sm[:, 1:2], in_=sm[:, 0:1])
-        nc.vector.tensor_tensor(out=sm[:, 2:3], in0=tot[:, 1:2], in1=tot[:, 2:3], op=ALU.add)
-        nc.vector.scalar_tensor_tensor(
-            out=sm[:, 3:4], in0=tot[:, 0:1], scalar=0.5, in1=sm[:, 2:3], op0=ALU.mult, op1=ALU.add
-        )
-        nc.vector.scalar_tensor_tensor(
-            out=sm[:, 4:5], in0=sm[:, 3:4], scalar=-0.5 * n_v, in1=sm[:, 1:2], op0=ALU.add, op1=ALU.mult
-        )
-        nc.vector.scalar_tensor_tensor(
-            out=sm[:, 5:6], in0=tot[:, 0:1], scalar=0.0, in1=sm[:, 4:5], op0=ALU.is_equal, op1=ALU.add
-        )
         s_ap = sm[:, 5:6]
 
-        for m in range(MT):
-            g = gpool.tile([P, D], BF16, name="g")
-            nc.sync.dma_start(out=g[:], in_=gflat[P * m : P * m + P, :])
-            gw = g[:].bitcast(F32)
-            gg = ggpool.tile([P, NPASS, P, 4], BF16, align_bytes=64, name="gg")
-            ggf = gg[:].bitcast(F32)
+        tr_ps = psum.tile([P, 130], F32, tag="b0", name="tr_ps")
+        cs_ps = psum.tile([P, NARROW], F32, tag="b1", name="cs_ps")
+
+        xts = {}
+        ggs = {}
+
+        def g_transpose(m):
+            gw = g_sb[m // 2][:, m % 2, :].bitcast(F32)
             for h in range(2):
-                xt = psum.tile([P, 2, 2, P], F32, tag="b%d" % (4 + (2 * m + h) % 4), name="xt")
+                xt = psum.tile([P, 2, 2, P], F32, tag="b%d" % G_BANK[m][h], name="xt")
+                xts[(m, h)] = xt
                 for cc in range(2):
                     for u in range(2):
                         w0 = 256 * (2 * h + cc) + P * u
                         nc.tensor.transpose(xt[:, cc, u, :], gw[:, w0 : w0 + P], ident[:])
+
+        def g_copy(m):
+            gg = ggpool.tile([P, NPASS, P, 4], BF16, align_bytes=64, name="gg")
+            ggs[m] = gg
+            ggf = gg[:].bitcast(F32)
+            for h in range(2):
                 nc.scalar.copy(
-                    out=ggf[:, 2 * h : 2 * h + 2, :, :], in_=xt[:].rearrange("p c u r -> p c r u")
+                    out=ggf[:, 2 * h : 2 * h + 2, :, :],
+                    in_=xts[(m, h)][:].rearrange("p c u r -> p c r u"),
                 )
+
+        def g_quant(m):
             nc.vector.quantize_mx(
                 out=gcodes[:, m, :].bitcast(E5),
                 scales=gscale[:, m, :],
-                in_=gg[:].rearrange("p c r t -> p (c r t)"),
+                in_=ggs[m][:].rearrange("p c r t -> p (c r t)"),
             )
 
-        post = ctx.enter_context(tc.tile_pool(name="post", bufs=3))
-        opool = ctx.enter_context(tc.tile_pool(name="opool", bufs=6))
-
-        def make_chunk(n, c):
+        def sign_or(j):
+            if j >= NCHUNK:
+                return
+            n, c = j // NPASS, j % NPASS
             cols = slice(512 * n, 512 * n + 512)
             tv = t_sb[c][:, :, cols].bitcast(I32)
             nc.vector.scalar_tensor_tensor(
@@ -182,55 +143,209 @@ def tile_ternarylinear_kernel(tc, x, weight, bias, grad_out, out):
                 op0=ALU.bitwise_and,
                 op1=ALU.bitwise_or,
             )
-            grp = post.tile([P, 512, 4], BF16, align_bytes=64, name="grp")
-            src = t_sb[c][:, :, cols]
-            vc = V_REGROUP
+
+        with tc.tile_pool(name="apool", bufs=1) as apool:
+            a_bufs = []
+            for k in range(3):
+                a_k = apool.tile([P, 32, 130], BF16, name="a%d" % k)
+                nc.vector.memset(a_k[:, :, 128:130], 1.0)
+                a_bufs.append(a_k)
+            junk = apool.tile([P, 2, 4, P], BF16, name="junk")
+            for i, (c, u, c0, ncol) in enumerate(PIECES):
+                nj = ncol // P
+                sj = S_BLOCKS[ncol]
+                rows = slice(2 * u, 2 * u + 2)
+                cols = slice(c0, c0 + ncol)
+                a = a_bufs[i % 3]
+                a4 = a[:, 0 : 2 * nj, 0:P].rearrange("p (e j) w -> p e j w", e=2)
+                nc.vector.tensor_scalar(
+                    out=a[:, 0 : 2 * nj, 0:P].bitcast(I32).rearrange("p (e j) w -> p e j w", e=2),
+                    in0=w_sb[c][:, rows, cols].bitcast(I32).rearrange("p e (j w) -> p e j w", w=64),
+                    scalar1=ABS_MASK,
+                    scalar2=None,
+                    op0=ALU.bitwise_and,
+                )
+                nc.scalar.activation(
+                    out=junk[:, :, 0:sj, :],
+                    in_=a4[:, :, 0:sj, :],
+                    func=ACT.Relu,
+                    bias=neghalf[:, 0:1],
+                    scale=1.0,
+                    accum_out=racc[:, i : i + 1],
+                )
+                nc.vector.tensor_scalar(
+                    out=t_sb[c][:, rows, cols].rearrange("p e (j w) -> p e j w", w=P),
+                    in0=a4,
+                    scalar1=0.5,
+                    scalar2=None,
+                    op0=ALU.is_gt,
+                )
+                for e in range(2):
+                    for j in range(nj):
+                        lhsT = t_sb[c][:, 2 * u + e, c0 + P * j : c0 + P * j + P]
+                        if j < sj:
+                            nc.tensor.matmul(
+                                cs_ps[:],
+                                lhsT=lhsT,
+                                rhs=ones_b[:, 0:NARROW],
+                                start=(i == 0 and e == 0 and j == 0),
+                                stop=(i == n_pc - 1 and e == 1 and j == sj - 1),
+                            )
+                        else:
+                            nc.tensor.matmul(
+                                tr_ps[:],
+                                lhsT=lhsT,
+                                rhs=a[:, e * nj + j, :],
+                                start=(i == 0 and e == 0 and j == sj),
+                                stop=(i == n_pc - 1 and e == 1 and j == nj - 1),
+                            )
+
+            g_transpose(0)
+            g_transpose(1)
+            sign_or(0)
+            g_copy(0)
+            nc.vector.scalar_tensor_tensor(
+                out=scr[:], in0=tr_ps[:, 0:P], scalar=1.0, in1=ident[:], op0=ALU.mult, op1=ALU.mult,
+                accum_out=st[:, 0:1],
+            )
+            nc.vector.tensor_reduce(out=st[:, 1:2], in_=racc[:], axis=AX.X, op=ALU.add)
+            nc.vector.tensor_copy(out=st[:, 2:3], in_=cs_ps[:, 0:1])
+            nc.vector.scalar_tensor_tensor(
+                out=st[:, 3:4], in0=st[:, 2:3], scalar=0.5, in1=st[:, 1:2], op0=ALU.mult, op1=ALU.add
+            )
+            nc.vector.tensor_tensor(out=stat[:, 1:2], in0=st[:, 3:4], in1=st[:, 0:1], op=ALU.add)
+            nc.vector.tensor_tensor(out=stat[:, 0:1], in0=tr_ps[:, 128:129], in1=st[:, 2:3], op=ALU.add)
+            tot_ps = psum.tile([P, 4], F32, tag="b2", name="tot_ps")
+            nc.tensor.matmul(tot_ps[:], lhsT=ones_f[:], rhs=stat[:], start=True, stop=True)
+            sign_or(1)
+            g_copy(1)
             nc.vector.tensor_scalar(
-                out=grp[:, 0:vc, :].rearrange("p (c i) t -> p c t i", i=4),
-                in0=src[:, :, 0:vc].rearrange("p t (c i) -> p c t i", i=4),
+                out=sm[:, 0:1], in0=tot_ps[:, 0:1], scalar1=1.0, scalar2=None, op0=ALU.max
+            )
+            nc.vector.reciprocal(out=sm[:, 1:2], in_=sm[:, 0:1])
+            nc.vector.tensor_tensor(out=sm[:, 4:5], in0=tot_ps[:, 1:2], in1=sm[:, 1:2], op=ALU.mult)
+            nc.vector.scalar_tensor_tensor(
+                out=sm[:, 5:6], in0=tot_ps[:, 0:1], scalar=0.0, in1=sm[:, 4:5], op0=ALU.is_equal, op1=ALU.add
+            )
+
+        post = ctx.enter_context(tc.tile_pool(name="post", bufs=3))
+        opool = ctx.enter_context(tc.tile_pool(name="opool", bufs=8))
+        grps = {}
+        accs = {}
+
+        def v_cols(j):
+            return V_COLS_RAMP if j < 4 else V_COLS
+
+        def grp_tile(j):
+            if j not in grps:
+                grp = post.tile([P, 512, 4], BF16, align_bytes=64, name="grp")
+                grps[j] = grp
+            return grps[j]
+
+        def regroup_v(j):
+            if j >= NCHUNK:
+                return
+            n, c = j // NPASS, j % NPASS
+            vc = v_cols(j)
+            nc.vector.tensor_scalar(
+                out=grp_tile(j)[:, 0:vc, :].rearrange("p (c i) t -> p c t i", i=4),
+                in0=t_sb[c][:, :, 512 * n : 512 * n + vc].rearrange("p t (c i) -> p c t i", i=4),
                 scalar1=s_ap,
                 scalar2=None,
                 op0=ALU.mult,
             )
+
+        def regroup_s(j):
+            if j >= NCHUNK:
+                return
+            n, c = j // NPASS, j % NPASS
+            vc = v_cols(j)
             nc.scalar.activation(
-                out=grp[:, vc:512, :].rearrange("p (c i) t -> p c t i", i=4),
-                in_=src[:, :, vc:512].rearrange("p t (c i) -> p c t i", i=4),
+                out=grp_tile(j)[:, vc:512, :].rearrange("p (c i) t -> p c t i", i=4),
+                in_=t_sb[c][:, :, 512 * n + vc : 512 * n + 512].rearrange("p t (c i) -> p c t i", i=4),
                 func=ACT.Copy,
                 scale=s_ap,
             )
+
+        def quant(j):
+            n, c = j // NPASS, j % NPASS
+            if n not in wcodes:
+                wc = share.tile([P, NPASS, 512], U32, tag="x", align_bytes=64, name="wcodes%d" % n)
+                wcodes[n] = wc
             nc.vector.quantize_mx(
-                out=wcodes[:, n, c, :].bitcast(E4),
+                out=wcodes[n][:, c, :].bitcast(E4),
                 scales=wscale[:, n, c, :],
-                in_=grp[:].rearrange("p w t -> p (w t)"),
+                in_=grps[j][:].rearrange("p w t -> p (w t)"),
             )
 
-        def mx_pass(acc, m, n, c):
-            nc.tensor.matmul_mx(
-                out=acc[:],
-                lhsT=gcodes[:, m, P * c : P * c + P].bitcast(E5),
-                lhsT_scale=gscale[:, m, P * c : P * c + P],
-                rhs=wcodes[:, n, c, :].bitcast(E4),
-                rhs_scale=wscale[:, n, c, :],
-                start=(c == 0),
-                stop=(c == NPASS - 1),
-            )
-
-        def finish(acc, m, n):
-            o = opool.tile([P, 512], F32, name="o")
-            nc.scalar.copy(out=o[:], in_=acc[:])
-            nc.sync.dma_start(out=oflat[P * m : P * m + P, 512 * n : 512 * n + 512], in_=o[:])
-
-        for n in range(NBLK):
-            groups = [range(0, 4), range(4, 8)] if n == 0 else [range(0, 8)]
-            for gi, ms in enumerate(groups):
-                accs = {}
-                for m in ms:
+        def mx(j, ms):
+            n, c = j // NPASS, j % NPASS
+            for m in ms:
+                if c == 0:
                     acc = psum.tile([P, 512], F32, tag="b%d" % m, name="acc")
                     accs[m] = acc
-                for c in range(NPASS):
-                    if gi == 0:
-                        make_chunk(n, c)
-                    for m in ms:
-                        mx_pass(accs[m], m, n, c)
-                for m in ms:
-                    finish(accs[m], m, n)
+                nc.tensor.matmul_mx(
+                    out=accs[m][:],
+                    lhsT=gcodes[:, m, P * c : P * c + P].bitcast(E5),
+                    lhsT_scale=gscale[:, m, P * c : P * c + P],
+                    rhs=wcodes[n][:, c, :].bitcast(E4),
+                    rhs_scale=wscale[:, n, c, :],
+                    start=(c == 0),
+                    stop=(c == NPASS - 1),
+                )
+
+        def on_vector(n, m):
+            return (m % 2 == 1) if n == NBLK - 1 else (m >= 7)
+
+        def evac(n, m):
+            o = opool.tile([P, 512], F32, name="o")
+            if on_vector(n, m):
+                nc.vector.tensor_copy(out=o[:], in_=accs[m][:])
+            else:
+                nc.scalar.copy(out=o[:], in_=accs[m][:])
+            nc.sync.dma_start(out=oflat[P * m : P * m + P, 512 * n : 512 * n + 512], in_=o[:])
+
+        regroup_v(0)
+        regroup_s(0)
+        for s in range(4):
+            if s == 3:
+                g_copy(6)
+                g_transpose(7)
+                g_copy(7)
+            elif s >= 1:
+                g_copy(2 * s)
+                g_copy(2 * s + 1)
+            if s < 2:
+                g_transpose(2 * s + 2)
+                g_transpose(2 * s + 3)
+            elif s == 2:
+                g_transpose(6)
+            g_quant(2 * s)
+            g_quant(2 * s + 1)
+            quant(s)
+            sign_or(s + 2)
+            regroup_s(s + 1)
+            regroup_v(s + 1)
+            for q in range(s):
+                mx(s, [2 * q, 2 * q + 1])
+            for c in range(s + 1):
+                mx(c, [2 * s, 2 * s + 1])
+        sign_or(6)
+        regroup_s(5)
+        for j in range(4, NCHUNK):
+            n, c = j // NPASS, j % NPASS
+            if c == 0:
+                for m in range(MT):
+                    if not on_vector(n - 1, m):
+                        evac(n - 1, m)
+            quant(j)
+            sign_or(j + LA_T)
+            regroup_s(j + LA_S)
+            regroup_v(j + LA_V)
+            if c == 0:
+                for m in range(MT):
+                    if on_vector(n - 1, m):
+                        evac(n - 1, m)
+            mx(j, range(MT))
+        for m in range(MT):
+            evac(NBLK - 1, m)

@@ -31,13 +31,11 @@ PIECES = (
     + [(c, u, 0, 2048) for c in range(4) for u in range(2) if (c, u) not in ((0, 0), (3, 1))]
     + [(3, 1, 0, 1024), (3, 1, 1024, 512), (3, 1, 1536, 512)]
 )
-S_BLOCKS = {2048: 4, 1024: 2, 512: 1}
-V_COLS_RAMP = 192
-V_COLS = 128
-LA_T = 3
-LA_S = 2
-LA_V = 1
-G_BANK = [(3, 4), (5, 6), (7, 3), (4, 5), (6, 7), (4, 5), (6, 7), (6, 7)]
+S_BLOCKS = {2048: 7, 1024: 3, 512: 2}
+N_S_PIECES = 8
+V_COLS_RAMP = 256
+V_COLS = 192
+G_BANK = [(3, 4), (5, 6), (7, 3), (4, 5), (6, 7), (3, 4), (5, 6), (7, 3)]
 
 
 def tile_ternarylinear_kernel(tc, x, weight, bias, grad_out, out):
@@ -48,7 +46,7 @@ def tile_ternarylinear_kernel(tc, x, weight, bias, grad_out, out):
 
     with ExitStack() as ctx:
         keep = ctx.enter_context(tc.tile_pool(name="keep", bufs=1))
-        share = ctx.enter_context(tc.tile_pool(name="share", bufs=3))
+        share = ctx.enter_context(tc.tile_pool(name="share", bufs=4))
         ggpool = ctx.enter_context(tc.tile_pool(name="ggpool", bufs=2))
         psum = ctx.enter_context(tc.psum_pool(name="psum", bufs=1))
 
@@ -65,16 +63,11 @@ def tile_ternarylinear_kernel(tc, x, weight, bias, grad_out, out):
             )
         g_sb = []
         for q in range(4):
-            if q < 3:
-                g_q = share.tile([P, 2, D], BF16, tag="x", align_bytes=64, name="g%d" % q)
-            else:
-                g_q = keep.tile([P, 2, D], BF16, name="g3")
+            g_q = share.tile([P, 2, D], BF16, tag="x", align_bytes=64, name="g%d" % q)
             nc.sync.dma_start(out=g_q[:], in_=gv[q])
             g_sb.append(g_q)
 
         wcodes = {}
-        wcodes0 = keep.tile([P, NPASS, 512], U32, align_bytes=64, name="wcodes0")
-        wcodes[0] = wcodes0
         wscale = keep.tile([P, NBLK, NPASS, 512], U8, align_bytes=64, name="wscale")
         gcodes = keep.tile([P, MT, 512], U32, align_bytes=64, name="gcodes")
         gscale = keep.tile([P, MT, 512], U8, align_bytes=64, name="gscale")
@@ -88,9 +81,9 @@ def tile_ternarylinear_kernel(tc, x, weight, bias, grad_out, out):
         neghalf = keep.tile([P, 1], F32, name="neghalf")
         nc.vector.memset(neghalf[:], -0.5)
         n_pc = len(PIECES)
-        racc = keep.tile([P, n_pc], F32, name="racc")
-        stat = keep.tile([P, 4], F32, name="stat")
-        nc.vector.memset(stat[:], 0.0)
+        racc = keep.tile([P, N_S_PIECES], F32, name="racc")
+        stat = keep.tile([P, 2], F32, name="stat")
+        stat_a = keep.tile([P, 2], F32, name="stat_a")
         st = keep.tile([P, 8], F32, name="st")
         scr = keep.tile([P, P], F32, name="scr")
         sm = keep.tile([P, 8], F32, name="sm")
@@ -98,6 +91,7 @@ def tile_ternarylinear_kernel(tc, x, weight, bias, grad_out, out):
 
         tr_ps = psum.tile([P, 130], F32, tag="b0", name="tr_ps")
         cs_ps = psum.tile([P, NARROW], F32, tag="b1", name="cs_ps")
+        tot_ps = psum.tile([P, 2], F32, tag="b2", name="tot_ps")
 
         xts = {}
         ggs = {}
@@ -150,10 +144,10 @@ def tile_ternarylinear_kernel(tc, x, weight, bias, grad_out, out):
                 a_k = apool.tile([P, 32, 130], BF16, name="a%d" % k)
                 nc.vector.memset(a_k[:, :, 128:130], 1.0)
                 a_bufs.append(a_k)
-            junk = apool.tile([P, 2, 4, P], BF16, name="junk")
+            junk = apool.tile([P, 2, 7, P], BF16, name="junk")
             for i, (c, u, c0, ncol) in enumerate(PIECES):
                 nj = ncol // P
-                sj = S_BLOCKS[ncol]
+                sj = S_BLOCKS[ncol] if i < N_S_PIECES else 0
                 rows = slice(2 * u, 2 * u + 2)
                 cols = slice(c0, c0 + ncol)
                 a = a_bufs[i % 3]
@@ -165,14 +159,15 @@ def tile_ternarylinear_kernel(tc, x, weight, bias, grad_out, out):
                     scalar2=None,
                     op0=ALU.bitwise_and,
                 )
-                nc.scalar.activation(
-                    out=junk[:, :, 0:sj, :],
-                    in_=a4[:, :, 0:sj, :],
-                    func=ACT.Relu,
-                    bias=neghalf[:, 0:1],
-                    scale=1.0,
-                    accum_out=racc[:, i : i + 1],
-                )
+                if sj > 0:
+                    nc.scalar.activation(
+                        out=junk[:, :, 0:sj, :],
+                        in_=a4[:, :, 0:sj, :],
+                        func=ACT.Relu,
+                        bias=neghalf[:, 0:1],
+                        scale=1.0,
+                        accum_out=racc[:, i : i + 1],
+                    )
                 nc.vector.tensor_scalar(
                     out=t_sb[c][:, rows, cols].rearrange("p e (j w) -> p e j w", w=P),
                     in0=a4,
@@ -189,7 +184,7 @@ def tile_ternarylinear_kernel(tc, x, weight, bias, grad_out, out):
                                 lhsT=lhsT,
                                 rhs=ones_b[:, 0:NARROW],
                                 start=(i == 0 and e == 0 and j == 0),
-                                stop=(i == n_pc - 1 and e == 1 and j == sj - 1),
+                                stop=(i == N_S_PIECES - 1 and e == 1 and j == sj - 1),
                             )
                         else:
                             nc.tensor.matmul(
@@ -199,36 +194,38 @@ def tile_ternarylinear_kernel(tc, x, weight, bias, grad_out, out):
                                 start=(i == 0 and e == 0 and j == sj),
                                 stop=(i == n_pc - 1 and e == 1 and j == nj - 1),
                             )
+                if i == N_S_PIECES - 1:
+                    nc.vector.tensor_reduce(out=st[:, 1:2], in_=racc[:], axis=AX.X, op=ALU.add)
+                    nc.vector.tensor_copy(out=stat_a[:, 0:1], in_=cs_ps[:, 0:1])
+                    nc.vector.scalar_tensor_tensor(
+                        out=stat_a[:, 1:2], in0=cs_ps[:, 0:1], scalar=0.5, in1=st[:, 1:2],
+                        op0=ALU.mult, op1=ALU.add,
+                    )
+                    nc.tensor.matmul(tot_ps[:], lhsT=ones_f[:], rhs=stat_a[:], start=True, stop=False)
 
-            g_transpose(0)
-            g_transpose(1)
-            sign_or(0)
-            g_copy(0)
             nc.vector.scalar_tensor_tensor(
                 out=scr[:], in0=tr_ps[:, 0:P], scalar=1.0, in1=ident[:], op0=ALU.mult, op1=ALU.mult,
-                accum_out=st[:, 0:1],
+                accum_out=stat[:, 1:2],
             )
-            nc.vector.tensor_reduce(out=st[:, 1:2], in_=racc[:], axis=AX.X, op=ALU.add)
-            nc.vector.tensor_copy(out=st[:, 2:3], in_=cs_ps[:, 0:1])
-            nc.vector.scalar_tensor_tensor(
-                out=st[:, 3:4], in0=st[:, 2:3], scalar=0.5, in1=st[:, 1:2], op0=ALU.mult, op1=ALU.add
-            )
-            nc.vector.tensor_tensor(out=stat[:, 1:2], in0=st[:, 3:4], in1=st[:, 0:1], op=ALU.add)
-            nc.vector.tensor_tensor(out=stat[:, 0:1], in0=tr_ps[:, 128:129], in1=st[:, 2:3], op=ALU.add)
-            tot_ps = psum.tile([P, 4], F32, tag="b2", name="tot_ps")
-            nc.tensor.matmul(tot_ps[:], lhsT=ones_f[:], rhs=stat[:], start=True, stop=True)
-            sign_or(1)
-            g_copy(1)
+            nc.vector.tensor_copy(out=stat[:, 0:1], in_=tr_ps[:, 128:129])
+            nc.tensor.matmul(tot_ps[:], lhsT=ones_f[:], rhs=stat[:], start=False, stop=True)
             nc.vector.tensor_scalar(
                 out=sm[:, 0:1], in0=tot_ps[:, 0:1], scalar1=1.0, scalar2=None, op0=ALU.max
             )
             nc.vector.reciprocal(out=sm[:, 1:2], in_=sm[:, 0:1])
-            nc.vector.tensor_tensor(out=sm[:, 4:5], in0=tot_ps[:, 1:2], in1=sm[:, 1:2], op=ALU.mult)
-            nc.vector.scalar_tensor_tensor(
-                out=sm[:, 5:6], in0=tot_ps[:, 0:1], scalar=0.0, in1=sm[:, 4:5], op0=ALU.is_equal, op1=ALU.add
+            nc.vector.tensor_scalar(
+                out=sm[:, 2:3], in0=tot_ps[:, 0:1], scalar1=1.0, scalar2=1.0, op0=ALU.min, op1=ALU.subtract
             )
+            nc.vector.scalar_tensor_tensor(
+                out=sm[:, 5:6], in0=tot_ps[:, 1:2], scalar=sm[:, 1:2], in1=sm[:, 2:3],
+                op0=ALU.mult, op1=ALU.subtract,
+            )
+            for m in range(MT):
+                g_transpose(m)
+                g_copy(m)
+                g_quant(m)
 
-        post = ctx.enter_context(tc.tile_pool(name="post", bufs=3))
+        post = ctx.enter_context(tc.tile_pool(name="post", bufs=4))
         opool = ctx.enter_context(tc.tile_pool(name="opool", bufs=8))
         grps = {}
         accs = {}
@@ -305,47 +302,13 @@ def tile_ternarylinear_kernel(tc, x, weight, bias, grad_out, out):
                 nc.scalar.copy(out=o[:], in_=accs[m][:])
             nc.sync.dma_start(out=oflat[P * m : P * m + P, 512 * n : 512 * n + 512], in_=o[:])
 
-        regroup_v(0)
-        regroup_s(0)
-        for s in range(4):
-            if s == 3:
-                g_copy(6)
-                g_transpose(7)
-                g_copy(7)
-            elif s >= 1:
-                g_copy(2 * s)
-                g_copy(2 * s + 1)
-            if s < 2:
-                g_transpose(2 * s + 2)
-                g_transpose(2 * s + 3)
-            elif s == 2:
-                g_transpose(6)
-            g_quant(2 * s)
-            g_quant(2 * s + 1)
-            quant(s)
-            sign_or(s + 2)
-            regroup_s(s + 1)
-            regroup_v(s + 1)
-            for q in range(s):
-                mx(s, [2 * q, 2 * q + 1])
-            for c in range(s + 1):
-                mx(c, [2 * s, 2 * s + 1])
-        sign_or(6)
-        regroup_s(5)
-        for j in range(4, NCHUNK):
+        for j in range(NCHUNK):
             n, c = j // NPASS, j % NPASS
-            if c == 0:
-                for m in range(MT):
-                    if not on_vector(n - 1, m):
-                        evac(n - 1, m)
+            sign_or(j)
+            regroup_s(j)
+            regroup_v(j)
             quant(j)
-            sign_or(j + LA_T)
-            regroup_s(j + LA_S)
-            regroup_v(j + LA_V)
-            if c == 0:
-                for m in range(MT):
-                    if on_vector(n - 1, m):
-                        evac(n - 1, m)
             mx(j, range(MT))
-        for m in range(MT):
-            evac(NBLK - 1, m)
+            if c == NPASS - 1:
+                for m in range(MT):
+                    evac(n, m)

@@ -33,6 +33,7 @@ PIECES = (
 )
 S_BLOCKS = {2048: 7, 1024: 3, 512: 2}
 N_S_PIECES = 8
+LAG = 2
 V_COLS_RAMP = 256
 V_COLS = 192
 G_BANK = [(3, 4), (5, 6), (7, 3), (4, 5), (6, 7), (3, 4), (5, 6), (7, 3)]
@@ -292,7 +293,7 @@ def tile_ternarylinear_kernel(tc, x, weight, bias, grad_out, out):
                 )
 
         def on_vector(n, m):
-            return (m % 2 == 1) if n == NBLK - 1 else (m >= 7)
+            return (m % 2 == 1) if n == NBLK - 1 else (m % 4 == 3)
 
         def evac(n, m):
             o = opool.tile([P, 512], F32, name="o")
@@ -302,13 +303,19 @@ def tile_ternarylinear_kernel(tc, x, weight, bias, grad_out, out):
                 nc.scalar.copy(out=o[:], in_=accs[m][:])
             nc.sync.dma_start(out=oflat[P * m : P * m + P, 512 * n : 512 * n + 512], in_=o[:])
 
-        for j in range(NCHUNK):
-            n, c = j // NPASS, j % NPASS
-            sign_or(j)
-            regroup_s(j)
-            regroup_v(j)
-            quant(j)
-            mx(j, range(MT))
-            if c == NPASS - 1:
-                for m in range(MT):
-                    evac(n, m)
+        for j in range(NCHUNK + LAG):
+            if j < NCHUNK:
+                sign_or(j)
+                regroup_s(j)
+                regroup_v(j)
+                quant(j)
+                mx(j, range(0, 4))
+                if j % NPASS == NPASS - 1:
+                    for m in range(0, 4):
+                        evac(j // NPASS, m)
+            jb = j - LAG
+            if jb >= 0:
+                mx(jb, range(4, MT))
+                if jb % NPASS == NPASS - 1:
+                    for m in range(4, MT):
+                        evac(jb // NPASS, m)

@@ -27,13 +27,14 @@ NARROW = 8
 ABS_MASK = 0x7FFF7FFF
 SIGN_MASK = -2147450880
 PIECES = (
-    [(0, 0, 0, 1024), (0, 0, 1024, 1024)]
+    [(0, 0, 0, 256), (0, 0, 256, 768), (0, 0, 1024, 1024)]
     + [(c, u, 0, 2048) for c in range(4) for u in range(2) if (c, u) not in ((0, 0), (3, 1))]
     + [(3, 1, 0, 1024), (3, 1, 1024, 512), (3, 1, 1536, 512)]
 )
-S_BLOCKS = {2048: 7, 1024: 3, 512: 2}
-N_S_PIECES = 8
+S_BLOCKS = {2048: 7, 1024: 3, 768: 2, 512: 2, 256: 1}
+N_S_PIECES = 9
 LAG = 2
+G_AFTER = {8: 0}
 V_COLS_RAMP = 256
 V_COLS = 192
 G_BANK = [(3, 4), (5, 6), (7, 3), (4, 5), (6, 7), (3, 4), (5, 6), (7, 3)]
@@ -58,15 +59,21 @@ def tile_ternarylinear_kernel(tc, x, weight, bias, grad_out, out):
             t_c = keep.tile([P, 4, D], BF16, name="t%d" % c)
             w_sb.append(w_c)
             t_sb.append(t_c)
-        for c, u, c0, ncol in PIECES:
-            nc.sync.dma_start(
-                out=w_sb[c][:, 2 * u : 2 * u + 2, c0 : c0 + ncol], in_=wv[c, u][:, :, c0 : c0 + ncol]
-            )
         g_sb = []
-        for q in range(4):
+
+        def g_load(q):
             g_q = share.tile([P, 2, D], BF16, tag="x", align_bytes=64, name="g%d" % q)
             nc.sync.dma_start(out=g_q[:], in_=gv[q])
             g_sb.append(g_q)
+
+        for i, (c, u, c0, ncol) in enumerate(PIECES):
+            nc.sync.dma_start(
+                out=w_sb[c][:, 2 * u : 2 * u + 2, c0 : c0 + ncol], in_=wv[c, u][:, :, c0 : c0 + ncol]
+            )
+            if i in G_AFTER:
+                g_load(G_AFTER[i])
+        for q in range(len(G_AFTER), 4):
+            g_load(q)
 
         wcodes = {}
         wscale = keep.tile([P, NBLK, NPASS, 512], U8, align_bytes=64, name="wscale")

from contextlib import ExitStack

import concourse.mybir as mybir
from concourse.masks import make_identity

FLOPS = 2 * 1024 * 2048 * 2048
BYTES = 2048 * 2048 * 2 + 1024 * 2048 * 2 + 1024 * 2048 * 4

BF16 = mybir.dt.bfloat16
F32 = mybir.dt.float32
I32 = mybir.dt.int32
U32 = mybir.dt.uint32
U8 = mybir.dt.uint8
E4 = mybir.dt.float8_e4m3fn_x4
E5 = mybir.dt.float8_e5m2_x4
ALU = mybir.AluOpType
ACT = mybir.ActivationFunctionType
AX = mybir.AxisListType

P = 128
D = 2048
NPASS = 4
NBLK = 4
NCHUNK = 16
MT = 8
NARROW = 8
ABS_MASK = 0x7FFF7FFF
SIGN_MASK = -2147450880
PIECES = (
    [(0, 0, 0, 256), (0, 0, 256, 768), (0, 0, 1024, 1024)]
    + [(c, u, 0, 2048) for c in range(4) for u in range(2) if (c, u) not in ((0, 0), (3, 1))]
    + [(3, 1, 0, 1024), (3, 1, 1024, 512), (3, 1, 1536, 512)]
)
S_BLOCKS = {2048: 7, 1024: 3, 768: 2, 512: 2, 256: 1}
N_S_PIECES = 9
LAG = 2
G_AFTER = {8: 0}
V_COLS_RAMP = 256
V_COLS = 192
G_BANK = [(3, 4), (5, 6), (7, 3), (4, 5), (6, 7), (3, 4), (5, 6), (7, 3)]


def tile_ternarylinear_kernel(tc, x, weight, bias, grad_out, out):
    nc = tc.nc
    wv = weight.rearrange("(c u p e) d -> c u p e d", c=NPASS, u=2, p=P, e=2)
    gv = grad_out.flatten_outer_dims().rearrange("(q t p) d -> q p t d", t=2, p=P)
    oflat = out.flatten_outer_dims()

    with ExitStack() as ctx:
        keep = ctx.enter_context(tc.tile_pool(name="keep", bufs=1))
        share = ctx.enter_context(tc.tile_pool(name="share", bufs=4))
        ggpool = ctx.enter_context(tc.tile_pool(name="ggpool", bufs=2))
        psum = ctx.enter_context(tc.psum_pool(name="psum", bufs=1))

        w_sb = []
        t_sb = []
        for c in range(NPASS):
            w_c = keep.tile([P, 4, D], BF16, name="w%d" % c)
            t_c = keep.tile([P, 4, D], BF16, name="t%d" % c)
            w_sb.append(w_c)
            t_sb.append(t_c)
        g_sb = []

        def g_load(q):
            g_q = share.tile([P, 2, D], BF16, tag="x", align_bytes=64, name="g%d" % q)
            nc.sync.dma_start(out=g_q[:], in_=gv[q])
            g_sb.append(g_q)

        for i, (c, u, c0, ncol) in enumerate(PIECES):
            nc.sync.dma_start(
                out=w_sb[c][:, 2 * u : 2 * u + 2, c0 : c0 + ncol], in_=wv[c, u][:, :, c0 : c0 + ncol]
            )
            if i in G_AFTER:
                g_load(G_AFTER[i])
        for q in range(len(G_AFTER), 4):
            g_load(q)

        wcodes = {}
        wscale = keep.tile([P, NBLK, NPASS, 512], U8, align_bytes=64, name="wscale")
        gcodes = keep.tile([P, MT, 512], U32, align_bytes=64, name="gcodes")
        gscale = keep.tile([P, MT, 512], U8, align_bytes=64, name="gscale")

        ident = keep.tile([P, P], F32, name="ident")
        make_identity(nc, ident[:])
        ones_f = keep.tile([P, P], F32, name="ones_f")
        nc.vector.memset(ones_f[:], 1.0)
        ones_b = keep.tile([P, 32], BF16, name="ones_b")
        nc.vector.memset(ones_b[:], 1.0)
        neghalf = keep.tile([P, 1], F32, name="neghalf")
        nc.vector.memset(neghalf[:], -0.5)
        n_pc = len(PIECES)
        racc = keep.tile([P, N_S_PIECES], F32, name="racc")
        stat = keep.tile([P, 2], F32, name="stat")
        stat_a = keep.tile([P, 2], F32, name="stat_a")
        st = keep.tile([P, 8], F32, name="st")
        scr = keep.tile([P, P], F32, name="scr")
        sm = keep.tile([P, 8], F32, name="sm")
        s_ap = sm[:, 5:6]

        tr_ps = psum.tile([P, 130], F32, tag="b0", name="tr_ps")
        cs_ps = psum.tile([P, NARROW], F32, tag="b1", name="cs_ps")
        tot_ps = psum.tile([P, 2], F32, tag="b2", name="tot_ps")

        xts = {}
        ggs = {}

        def g_transpose(m):
            gw = g_sb[m // 2][:, m % 2, :].bitcast(F32)
            for h in range(2):
                xt = psum.tile([P, 2, 2, P], F32, tag="b%d" % G_BANK[m][h], name="xt")
                xts[(m, h)] = xt
                for cc in range(2):
                    for u in range(2):
                        w0 = 256 * (2 * h + cc) + P * u
                        nc.tensor.transpose(xt[:, cc, u, :], gw[:, w0 : w0 + P], ident[:])

        def g_copy(m):
            gg = ggpool.tile([P, NPASS, P, 4], BF16, align_bytes=64, name="gg")
            ggs[m] = gg
            ggf = gg[:].bitcast(F32)
            for h in range(2):
                nc.scalar.copy(
                    out=ggf[:, 2 * h : 2 * h + 2, :, :],
                    in_=xts[(m, h)][:].rearrange("p c u r -> p c r u"),
                )

        def g_quant(m):
            nc.vector.quantize_mx(
                out=gcodes[:, m, :].bitcast(E5),
                scales=gscale[:, m, :],
                in_=ggs[m][:].rearrange("p c r t -> p (c r t)"),
            )

        def sign_or(j):
            if j >= NCHUNK:
                return
            n, c = j // NPASS, j % NPASS
            cols = slice(512 * n, 512 * n + 512)
            tv = t_sb[c][:, :, cols].bitcast(I32)
            nc.vector.scalar_tensor_tensor(
                out=tv,
                in0=w_sb[c][:, :, cols].bitcast(I32),
                scalar=SIGN_MASK,
                in1=tv,
                op0=ALU.bitwise_and,
                op1=ALU.bitwise_or,
            )

        with tc.tile_pool(name="apool", bufs=1) as apool:
            a_bufs = []
            for k in range(3):
                a_k = apool.tile([P, 32, 130], BF16, name="a%d" % k)
                nc.vector.memset(a_k[:, :, 128:130], 1.0)
                a_bufs.append(a_k)
            junk = apool.tile([P, 2, 7, P], BF16, name="junk")
            for i, (c, u, c0, ncol) in enumerate(PIECES):
                nj = ncol // P
                sj = S_BLOCKS[ncol] if i < N_S_PIECES else 0
                rows = slice(2 * u, 2 * u + 2)
                cols = slice(c0, c0 + ncol)
                a = a_bufs[i % 3]
                a4 = a[:, 0 : 2 * nj, 0:P].rearrange("p (e j) w -> p e j w", e=2)
                nc.vector.tensor_scalar(
                    out=a[:, 0 : 2 * nj, 0:P].bitcast(I32).rearrange("p (e j) w -> p e j w", e=2),
                    in0=w_sb[c][:, rows, cols].bitcast(I32).rearrange("p e (j w) -> p e j w", w=64),
                    scalar1=ABS_MASK,
                    scalar2=None,
                    op0=ALU.bitwise_and,
                )
                if sj > 0:
                    nc.scalar.activation(
                        out=junk[:, :, 0:sj, :],
                        in_=a4[:, :, 0:sj, :],
                        func=ACT.Relu,
                        bias=neghalf[:, 0:1],
                        scale=1.0,
                        accum_out=racc[:, i : i + 1],
                    )
                nc.vector.tensor_scalar(
                    out=t_sb[c][:, rows, cols].rearrange("p e (j w) -> p e j w", w=P),
                    in0=a4,
                    scalar1=0.5,
                    scalar2=None,
                    op0=ALU.is_gt,
                )
                for e in range(2):
                    for j in range(nj):
                        lhsT = t_sb[c][:, 2 * u + e, c0 + P * j : c0 + P * j + P]
                        if j < sj:
                            nc.tensor.matmul(
                                cs_ps[:],
                                lhsT=lhsT,
                                rhs=ones_b[:, 0:NARROW],
                                start=(i == 0 and e == 0 and j == 0),
                                stop=(i == N_S_PIECES - 1 and e == 1 and j == sj - 1),
                            )
                        else:
                            nc.tensor.matmul(
                                tr_ps[:],
                                lhsT=lhsT,
                                rhs=a[:, e * nj + j, :],
                                start=(i == 0 and e == 0 and j == sj),
                                stop=(i == n_pc - 1 and e == 1 and j == nj - 1),
                            )
                if i == N_S_PIECES - 1:
                    nc.vector.tensor_reduce(out=st[:, 1:2], in_=racc[:], axis=AX.X, op=ALU.add)
                    nc.vector.tensor_copy(out=stat_a[:, 0:1], in_=cs_ps[:, 0:1])
                    nc.vector.scalar_tensor_tensor(
                        out=stat_a[:, 1:2], in0=cs_ps[:, 0:1], scalar=0.5, in1=st[:, 1:2],
                        op0=ALU.mult, op1=ALU.add,
                    )
                    nc.tensor.matmul(tot_ps[:], lhsT=ones_f[:], rhs=stat_a[:], start=True, stop=False)

            nc.vector.scalar_tensor_tensor(
                out=scr[:], in0=tr_ps[:, 0:P], scalar=1.0, in1=ident[:], op0=ALU.mult, op1=ALU.mult,
                accum_out=stat[:, 1:2],
            )
            nc.vector.tensor_copy(out=stat[:, 0:1], in_=tr_ps[:, 128:129])
            nc.tensor.matmul(tot_ps[:], lhsT=ones_f[:], rhs=stat[:], start=False, stop=True)
            nc.vector.tensor_scalar(
                out=sm[:, 0:1], in0=tot_ps[:, 0:1], scalar1=1.0, scalar2=None, op0=ALU.max
            )
            nc.vector.reciprocal(out=sm[:, 1:2], in_=sm[:, 0:1])
            nc.vector.tensor_scalar(
                out=sm[:, 2:3], in0=tot_ps[:, 0:1], scalar1=1.0, scalar2=1.0, op0=ALU.min, op1=ALU.subtract
            )
            nc.vector.scalar_tensor_tensor(
                out=sm[:, 5:6], in0=tot_ps[:, 1:2], scalar=sm[:, 1:2], in1=sm[:, 2:3],
                op0=ALU.mult, op1=ALU.subtract,
            )
            for m in range(MT):
                g_transpose(m)
                g_copy(m)
                g_quant(m)

        post = ctx.enter_context(tc.tile_pool(name="post", bufs=4))
        opool = ctx.enter_context(tc.tile_pool(name="opool", bufs=8))
        grps = {}
        accs = {}

        def v_cols(j):
            return V_COLS_RAMP if j < 4 else V_COLS

        def grp_tile(j):
            if j not in grps:
                grp = post.tile([P, 512, 4], BF16, align_bytes=64, name="grp")
                grps[j] = grp
            return grps[j]

        def regroup_v(j):
            if j >= NCHUNK:
                return
            n, c = j // NPASS, j % NPASS
            vc = v_cols(j)
            nc.vector.tensor_scalar(
                out=grp_tile(j)[:, 0:vc, :].rearrange("p (c i) t -> p c t i", i=4),
                in0=t_sb[c][:, :, 512 * n : 512 * n + vc].rearrange("p t (c i) -> p c t i", i=4),
                scalar1=s_ap,
                scalar2=None,
                op0=ALU.mult,
            )

        def regroup_s(j):
            if j >= NCHUNK:
                return
            n, c = j // NPASS, j % NPASS
            vc = v_cols(j)
            nc.scalar.activation(
                out=grp_tile(j)[:, vc:512, :].rearrange("p (c i) t -> p c t i", i=4),
                in_=t_sb[c][:, :, 512 * n + vc : 512 * n + 512].rearrange("p t (c i) -> p c t i", i=4),
                func=ACT.Copy,
                scale=s_ap,
            )

        def quant(j):
            n, c = j // NPASS, j % NPASS
            if n not in wcodes:
                wc = share.tile([P, NPASS, 512], U32, tag="x", align_bytes=64, name="wcodes%d" % n)
                wcodes[n] = wc
            nc.vector.quantize_mx(
                out=wcodes[n][:, c, :].bitcast(E4),
                scales=wscale[:, n, c, :],
                in_=grps[j][:].rearrange("p w t -> p (w t)"),
            )

        def mx(j, ms):
            n, c = j // NPASS, j % NPASS
            for m in ms:
                if c == 0:
                    acc = psum.tile([P, 512], F32, tag="b%d" % m, name="acc")
                    accs[m] = acc
                nc.tensor.matmul_mx(
                    out=accs[m][:],
                    lhsT=gcodes[:, m, P * c : P * c + P].bitcast(E5),
                    lhsT_scale=gscale[:, m, P * c : P * c + P],
                    rhs=wcodes[n][:, c, :].bitcast(E4),
                    rhs_scale=wscale[:, n, c, :],
                    start=(c == 0),
                    stop=(c == NPASS - 1),
                )

        def on_vector(n, m):
            return (m % 2 == 1) if n == NBLK - 1 else (m % 4 == 3)

        def evac(n, m):
            o = opool.tile([P, 512], F32, name="o")
            if on_vector(n, m):
                nc.vector.tensor_copy(out=o[:], in_=accs[m][:])
            else:
                nc.scalar.copy(out=o[:], in_=accs[m][:])
            nc.sync.dma_start(out=oflat[P * m : P * m + P, 512 * n : 512 * n + 512], in_=o[:])

        for j in range(NCHUNK + LAG):
            if j < NCHUNK:
                sign_or(j)
                regroup_s(j)
                regroup_v(j)
                quant(j)
                mx(j, range(0, 4))
                if j % NPASS == NPASS - 1:
                    for m in range(0, 4):
                        evac(j // NPASS, m)
            jb = j - LAG
            if jb >= 0:
                mx(jb, range(4, MT))
                if jb % NPASS == NPASS - 1:
                    for m in range(4, MT):
                        evac(jb // NPASS, m)
